import numpy as np
import ml_dtypes


def mxq(x, axis, fmt="e4m3"):
    dtype, down = {"e4m3": (ml_dtypes.float8_e4m3fn, 7), "e5m2": (ml_dtypes.float8_e5m2, 14)}[fmt]
    v = np.moveaxis(np.asarray(x, np.float32).astype(ml_dtypes.bfloat16).astype(np.float64), axis, -1)
    blocks = v.reshape(v.shape[:-1] + (-1, 32))
    amax = np.abs(blocks).max(-1, keepdims=True)
    byte = np.maximum(np.where(amax > 0, np.frexp(amax)[1] - 1 + 127, 0) - down, 1)
    scale = np.exp2(byte - 127.0)
    codes = (blocks / scale).astype(np.float32).astype(dtype).astype(np.float64)
    return np.moveaxis((codes * scale).reshape(v.shape), -1, axis)


WIDE = False


def mx_kscale(k):
    if not WIDE:
        return np.ones(k)
    levels = np.array([20, -20, 10, -10, 0])
    a = np.random.permutation(np.resize(levels, k // 512 * 4)).reshape(k // 512, 4)
    idx = np.arange(k)
    return np.exp2(a[idx // 512, idx % 128 // 32])


BF16 = ml_dtypes.bfloat16


def bf(x):
    return np.asarray(x, np.float32).astype(BF16)


def f64(x):
    return np.asarray(x).astype(np.float64)


B, H, W, C, UP = 1, 64, 64, 1024, 2
K = C // UP


def setup_inputs():
    u = mx_kscale(K)
    x = np.random.standard_normal((B, H * W, C))
    w = np.random.standard_normal((K, K)) / np.sqrt(K) / u[None, :]
    g = (np.random.standard_normal((B, H * W * UP, K))
         * np.exp2(np.random.randint(-12, 1, (B, H * W * UP, 1))) * 8.0 * u)
    return {"x": bf(x), "w": bf(w), "grad_out": bf(g)}


def reference(x, w, grad_out):
    g = f64(grad_out)
    gxi = mxq(g, 2, "e5m2") @ mxq(f64(w), 1, "e4m3").T
    gxi = gxi.reshape(B, H, UP, W, K)
    return gxi.transpose(0, 1, 3, 2, 4).reshape(B, H * W, C)

@@ -1,0 +1,140 @@
+from contextlib import ExitStack
+
+import concourse.mybir as mybir
+from concourse.masks import make_identity
+
+F32 = mybir.dt.float32
+BF16 = mybir.dt.bfloat16
+U32 = mybir.dt.uint32
+U8 = mybir.dt.uint8
+E4M3X4 = mybir.dt.float8_e4m3fn_x4
+E5M2X4 = mybir.dt.float8_e5m2_x4
+
+P = 128
+K = 512
+TOKENS = 8192
+T_PER_P = 32
+GROUP_T = 4
+N_GROUPS = T_PER_P // GROUP_T
+PASSES = 2 * GROUP_T
+LOAD_CUTS = ((0, 4), (4, 8), (8, 16), (16, 32))
+
+FLOPS = 2 * TOKENS * K * K
+BYTES = TOKENS * K * 2 + K * K * 2 + TOKENS * K * 4
+
+
+def tile_patch_expanding_t_kernel(tc, x, w, grad_out, out):
+    nc = tc.nc
+    g_view = grad_out.rearrange("b (q r h t) k -> h (b q) r (t k)", r=2, h=2, t=T_PER_P)
+    out_view = out.rearrange("b (p t) c -> (b p) (t c)", t=T_PER_P)
+    w_view = w.rearrange("(a p) k -> p a k", p=P)
+
+    with ExitStack() as ctx:
+        keep = ctx.enter_context(tc.tile_pool(name="keep", bufs=1))
+        stage = ctx.enter_context(tc.tile_pool(name="stage", bufs=3))
+        res = ctx.enter_context(tc.tile_pool(name="res", bufs=6))
+        tp_pool = ctx.enter_context(tc.psum_pool(name="tp", bufs=4))
+        acc_pool = ctx.enter_context(tc.psum_pool(name="acc", bufs=4))
+        ctx.enter_context(tc.manual_schedule())
+
+        w_sb = keep.tile([P, 4 * K], BF16, name="w_sb")
+        nc.sync.dma_start(out=w_sb[:].rearrange("p (a k) -> p a k", a=4), in_=w_view)
+        g_tiles = {}
+        for c, (t0, t1) in enumerate(LOAD_CUTS):
+            g_sb = keep.tile([P, 2, (t1 - t0) * K], BF16, name="g_sb_%d" % c)
+            for h in range(2):
+                nc.sync.dma_start(out=g_sb[h:P:2, :, :], in_=g_view[h, :, :, t0 * K : t1 * K])
+            g_tiles[c] = g_sb
+
+        ident = keep.tile([P, P], F32, name="ident")
+        make_identity(nc, ident[:])
+
+        def g_words(r, t):
+            for c, (t0, t1) in enumerate(LOAD_CUTS):
+                if t0 <= t < t1:
+                    return g_tiles[c][:, r, :].bitcast(F32), (t - t0) * (K // 2)
+            raise ValueError("t out of range")
+
+        def regroup(copy, bank, grouped, b, m):
+            dst = grouped[:].bitcast(F32).rearrange("p (m n u) -> p m n u", m=m, u=2)
+            src = bank[:].rearrange("p (m u) n -> p m n u", u=2)
+            copy(out=dst[:, 2 * b : 2 * b + 2, :, :], in_=src)
+
+        w_words = w_sb[:].bitcast(F32)
+        w_grouped = keep.tile([P, 4 * K], BF16, name="w_grouped", align_bytes=64)
+        w_codes = keep.tile([P, K], U32, name="w_codes", align_bytes=64)
+        w_scales = keep.tile([P, K], U8, name="w_scales", align_bytes=64)
+        for b in range(2):
+            bank = tp_pool.tile([P, 4, P], F32, tag="tp")
+            for j in range(4):
+                col = (4 * b + j) * P
+                nc.tensor.transpose(bank[:, j, :], w_words[:, col : col + P], ident[:])
+            regroup(nc.vector.tensor_copy if b == 0 else nc.scalar.copy, bank, w_grouped, b, 4)
+        nc.vector.quantize_mx(out=w_codes[:].bitcast(E4M3X4), scales=w_scales[:], in_=w_grouped[:])
+
+        banks = {}
+        grouped = {}
+        codes = {}
+        scales = {}
+
+        def transposes(g):
+            for b in range(GROUP_T):
+                bank = tp_pool.tile([P, 4, P], F32, tag="tp")
+                for r in range(2):
+                    words, col = g_words(r, GROUP_T * g + b)
+                    for u in range(2):
+                        nc.tensor.transpose(
+                            bank[:, 2 * r + u, :], words[:, col + P * u : col + P * (u + 1)], ident[:]
+                        )
+                banks[(g, b)] = bank
+
+        def copies(g, bs, both):
+            if g not in grouped:
+                grouped_t = stage.tile([P, PASSES * K], BF16, tag="grouped", align_bytes=64)
+                grouped[g] = grouped_t
+            for b in bs:
+                copy = nc.scalar.copy if (both and b % 2 == 1) else nc.vector.tensor_copy
+                regroup(copy, banks[(g, b)], grouped[g], b, PASSES)
+
+        def quantise(g):
+            codes_t = stage.tile([P, PASSES * P], U32, tag="codes", align_bytes=64)
+            scales_t = stage.tile([P, PASSES * P], U8, tag="scales", align_bytes=64)
+            nc.vector.quantize_mx(out=codes_t[:].bitcast(E5M2X4), scales=scales_t[:], in_=grouped[g][:])
+            codes[g] = codes_t
+            scales[g] = scales_t
+
+        def one_pass(g, m, o_sb, copy):
+            acc = acc_pool.tile([P, K], F32, tag="acc")
+            cols = slice(m * P, (m + 1) * P)
+            nc.tensor.matmul_mx(
+                out=acc[:],
+                lhsT=codes[g][:, cols].bitcast(E5M2X4),
+                lhsT_scale=scales[g][:, cols],
+                rhs=w_codes[:].bitcast(E4M3X4),
+                rhs_scale=w_scales[:],
+                start=True,
+                stop=True,
+            )
+            copy(out=o_sb[:, m * K : (m + 1) * K], in_=acc[:])
+
+        transposes(0)
+        copies(0, range(4), True)
+        transposes(1)
+        quantise(0)
+        copies(1, range(4), True)
+
+        for s in range(N_GROUPS):
+            if s + 2 < N_GROUPS:
+                transposes(s + 2)
+            if s + 1 < N_GROUPS:
+                quantise(s + 1)
+            if s + 2 < N_GROUPS:
+                copies(s + 2, (0, 1), False)
+            o_sb = res.tile([P, PASSES * K], F32, tag="o_sb")
+            one_pass(s, 0, o_sb, nc.scalar.copy)
+            one_pass(s, 1, o_sb, nc.vector.tensor_copy)
+            if s + 2 < N_GROUPS:
+                copies(s + 2, (2, 3), False)
+            for m in range(2, PASSES):
+                one_pass(s, m, o_sb, nc.scalar.copy)
+            nc.sync.dma_start(out=out_view[:, s * PASSES * K : (s + 1) * PASSES * K], in_=o_sb[:])

@@ -17,7 +17,7 @@ T_PER_P = 32
 GROUP_T = 4
 N_GROUPS = T_PER_P // GROUP_T
 PASSES = 2 * GROUP_T
-LOAD_CUTS = ((0, 4), (4, 8), (8, 16), (16, 32))
+LOAD_CUTS = ((0, 4), (4, 8), (8, 12), (12, 20), (20, 32))
 
 FLOPS = 2 * TOKENS * K * K
 BYTES = TOKENS * K * 2 + K * K * 2 + TOKENS * K * 4
@@ -27,7 +27,7 @@ def tile_patch_expanding_t_kernel(tc, x, w, grad_out, out):
     nc = tc.nc
     g_view = grad_out.rearrange("b (q r h t) k -> h (b q) r (t k)", r=2, h=2, t=T_PER_P)
     out_view = out.rearrange("b (p t) c -> (b p) (t c)", t=T_PER_P)
-    w_view = w.rearrange("(a p) k -> p a k", p=P)
+    w_view = w.rearrange("(p a) k -> p (a k)", a=4)
 
     with ExitStack() as ctx:
         keep = ctx.enter_context(tc.tile_pool(name="keep", bufs=1))
@@ -38,7 +38,7 @@ def tile_patch_expanding_t_kernel(tc, x, w, grad_out, out):
         ctx.enter_context(tc.manual_schedule())
 
         w_sb = keep.tile([P, 4 * K], BF16, name="w_sb")
-        nc.sync.dma_start(out=w_sb[:].rearrange("p (a k) -> p a k", a=4), in_=w_view)
+        nc.sync.dma_start(out=w_sb[:], in_=w_view)
         g_tiles = {}
         for c, (t0, t1) in enumerate(LOAD_CUTS):
             g_sb = keep.tile([P, 2, (t1 - t0) * K], BF16, name="g_sb_%d" % c)
@@ -69,7 +69,10 @@ def tile_patch_expanding_t_kernel(tc, x, w, grad_out, out):
             for j in range(4):
                 col = (4 * b + j) * P
                 nc.tensor.transpose(bank[:, j, :], w_words[:, col : col + P], ident[:])
-            regroup(nc.vector.tensor_copy if b == 0 else nc.scalar.copy, bank, w_grouped, b, 4)
+            nc.vector.tensor_copy(
+                out=w_grouped[:].bitcast(F32).rearrange("p (n a u) -> p n a u", a=4, u=2)[:, :, 2 * b : 2 * b + 2, :],
+                in_=bank[:].rearrange("p (m u) n -> p n m u", u=2),
+            )
         nc.vector.quantize_mx(out=w_codes[:].bitcast(E4M3X4), scales=w_scales[:], in_=w_grouped[:])
 
         banks = {}

@@ -138,6 +138,13 @@ def tile_patch_expanding_t_kernel(tc, x, w, grad_out, out):
             one_pass(s, 1, o_sb, nc.vector.tensor_copy)
             if s + 2 < N_GROUPS:
                 copies(s + 2, (2, 3), False)
+            base = s * PASSES * K
+            half = PASSES * K // 2
             for m in range(2, PASSES):
                 one_pass(s, m, o_sb, nc.scalar.copy)
-            nc.sync.dma_start(out=out_view[:, s * PASSES * K : (s + 1) * PASSES * K], in_=o_sb[:])
+                if s >= N_GROUPS - 2 and m == PASSES // 2 - 1:
+                    nc.sync.dma_start(out=out_view[:, base : base + half], in_=o_sb[:, 0:half])
+            if s >= N_GROUPS - 2:
+                nc.sync.dma_start(out=out_view[:, base + half : base + 2 * half], in_=o_sb[:, half : 2 * half])
+            else:
+                nc.sync.dma_start(out=out_view[:, base : base + 2 * half], in_=o_sb[:])

@@ -25,7 +25,7 @@ BYTES = TOKENS * K * 2 + K * K * 2 + TOKENS * K * 4
 
 def tile_patch_expanding_t_kernel(tc, x, w, grad_out, out):
     nc = tc.nc
-    g_view = grad_out.rearrange("b (q r h t) k -> h (b q) r (t k)", r=2, h=2, t=T_PER_P)
+    g_view = grad_out.rearrange("b (p h t) k -> (b p) h (t k)", h=2, t=T_PER_P)
     out_view = out.rearrange("b (p t) c -> (b p) (t c)", t=T_PER_P)
     w_view = w.rearrange("(p a) k -> p (a k)", a=4)
 
@@ -42,22 +42,21 @@ def tile_patch_expanding_t_kernel(tc, x, w, grad_out, out):
         g_tiles = {}
         for c, (t0, t1) in enumerate(LOAD_CUTS):
             g_sb = keep.tile([P, 2, (t1 - t0) * K], BF16, name="g_sb_%d" % c)
-            for h in range(2):
-                nc.sync.dma_start(out=g_sb[h:P:2, :, :], in_=g_view[h, :, :, t0 * K : t1 * K])
+            nc.sync.dma_start(out=g_sb[:], in_=g_view[:, :, t0 * K : t1 * K])
             g_tiles[c] = g_sb
 
         ident = keep.tile([P, P], F32, name="ident")
         make_identity(nc, ident[:])
 
-        def g_words(r, t):
+        def g_words(h, t):
             for c, (t0, t1) in enumerate(LOAD_CUTS):
                 if t0 <= t < t1:
-                    return g_tiles[c][:, r, :].bitcast(F32), (t - t0) * (K // 2)
+                    return g_tiles[c][:, h, :].bitcast(F32), (t - t0) * (K // 2)
             raise ValueError("t out of range")
 
         def regroup(copy, bank, grouped, b, m):
-            dst = grouped[:].bitcast(F32).rearrange("p (m n u) -> p m n u", m=m, u=2)
-            src = bank[:].rearrange("p (m u) n -> p m n u", u=2)
+            dst = grouped[:].bitcast(F32).rearrange("p (m i v) -> p m i v", m=m, v=4)
+            src = bank[:].rearrange("p v (i r) -> p r i v", r=2)
             copy(out=dst[:, 2 * b : 2 * b + 2, :, :], in_=src)
 
         w_words = w_sb[:].bitcast(F32)
@@ -83,11 +82,11 @@ def tile_patch_expanding_t_kernel(tc, x, w, grad_out, out):
         def transposes(g):
             for b in range(GROUP_T):
                 bank = tp_pool.tile([P, 4, P], F32, tag="tp")
-                for r in range(2):
-                    words, col = g_words(r, GROUP_T * g + b)
+                for h in range(2):
+                    words, col = g_words(h, GROUP_T * g + b)
                     for u in range(2):
                         nc.tensor.transpose(
-                            bank[:, 2 * r + u, :], words[:, col + P * u : col + P * (u + 1)], ident[:]
+                            bank[:, 2 * h + u, :], words[:, col + P * u : col + P * (u + 1)], ident[:]
                         )
                 banks[(g, b)] = bank
 

@@ -16,8 +16,10 @@ TOKENS = 8192
 T_PER_P = 32
 GROUP_T = 4
 N_GROUPS = T_PER_P // GROUP_T
+VECTOR_PASS = 5
 PASSES = 2 * GROUP_T
-LOAD_CUTS = ((0, 4), (4, 8), (8, 12), (12, 20), (20, 32))
+RUN = 2 * GROUP_T
+LOAD_CUTS = ((0, 1), (1, 2), (2, 3), (3, 5), (5, 8))
 
 FLOPS = 2 * TOKENS * K * K
 BYTES = TOKENS * K * 2 + K * K * 2 + TOKENS * K * 4
@@ -25,8 +27,8 @@ BYTES = TOKENS * K * 2 + K * K * 2 + TOKENS * K * 4
 
 def tile_patch_expanding_t_kernel(tc, x, w, grad_out, out):
     nc = tc.nc
-    g_view = grad_out.rearrange("b (p h t) k -> (b p) h (t k)", h=2, t=T_PER_P)
-    out_view = out.rearrange("b (p t) c -> (b p) (t c)", t=T_PER_P)
+    g_view = grad_out.rearrange("b (g p t) k -> (b p) g (t k)", p=P, t=RUN)
+    out_view = out.rearrange("b (g p t) c -> g (b p) (t c)", p=P, t=GROUP_T)
     w_view = w.rearrange("(p a) k -> p (a k)", a=4)
 
     with ExitStack() as ctx:
@@ -40,23 +42,24 @@ def tile_patch_expanding_t_kernel(tc, x, w, grad_out, out):
         w_sb = keep.tile([P, 4 * K], BF16, name="w_sb")
         nc.sync.dma_start(out=w_sb[:], in_=w_view)
         g_tiles = {}
-        for c, (t0, t1) in enumerate(LOAD_CUTS):
-            g_sb = keep.tile([P, 2, (t1 - t0) * K], BF16, name="g_sb_%d" % c)
-            nc.sync.dma_start(out=g_sb[:], in_=g_view[:, :, t0 * K : t1 * K])
-            g_tiles[c] = g_sb
+        for g_first, g_end in LOAD_CUTS:
+            g_sb = keep.tile([P, g_end - g_first, RUN * K], BF16, name="g_sb_%d" % g_first)
+            nc.sync.dma_start(out=g_sb[:], in_=g_view[:, g_first:g_end, :])
+            for g in range(g_first, g_end):
+                g_tiles[g] = g_sb[:, g - g_first, :].bitcast(F32)
 
         ident = keep.tile([P, P], F32, name="ident")
         make_identity(nc, ident[:])
 
-        def g_words(h, t):
-            for c, (t0, t1) in enumerate(LOAD_CUTS):
-                if t0 <= t < t1:
-                    return g_tiles[c][:, h, :].bitcast(F32), (t - t0) * (K // 2)
-            raise ValueError("t out of range")
+        perm = keep.tile([P, P], F32, name="perm")
+        nc.vector.tensor_copy(
+            out=perm[:].rearrange("p (r i j) -> p r i j", r=2, i=8),
+            in_=ident[:].rearrange("p (i r j) -> p r i j", i=8, r=2),
+        )
 
         def regroup(copy, bank, grouped, b, m):
-            dst = grouped[:].bitcast(F32).rearrange("p (m i v) -> p m i v", m=m, v=4)
-            src = bank[:].rearrange("p v (i r) -> p r i v", r=2)
+            dst = grouped[:].bitcast(F32).rearrange("p (m n v) -> p m n v", m=m, v=4)
+            src = bank[:].rearrange("p v (r n) -> p r n v", r=2)
             copy(out=dst[:, 2 * b : 2 * b + 2, :, :], in_=src)
 
         w_words = w_sb[:].bitcast(F32)
@@ -79,15 +82,13 @@ def tile_patch_expanding_t_kernel(tc, x, w, grad_out, out):
         codes = {}
         scales = {}
 
-        def transposes(g):
-            for b in range(GROUP_T):
+        def transposes(g, bs):
+            for b in bs:
                 bank = tp_pool.tile([P, 4, P], F32, tag="tp")
                 for h in range(2):
-                    words, col = g_words(h, GROUP_T * g + b)
                     for u in range(2):
-                        nc.tensor.transpose(
-                            bank[:, 2 * h + u, :], words[:, col + P * u : col + P * (u + 1)], ident[:]
-                        )
+                        col = (GROUP_T * h + b) * (K // 2) + P * u
+                        nc.tensor.transpose(bank[:, 2 * h + u, :], g_tiles[g][:, col : col + P], perm[:])
                 banks[(g, b)] = bank
 
         def copies(g, bs, both):
@@ -119,31 +120,31 @@ def tile_patch_expanding_t_kernel(tc, x, w, grad_out, out):
             )
             copy(out=o_sb[:, m * K : (m + 1) * K], in_=acc[:])
 
-        transposes(0)
+        transposes(0, range(4))
         copies(0, range(4), True)
-        transposes(1)
+        transposes(1, range(4))
         quantise(0)
         copies(1, range(4), True)
 
         for s in range(N_GROUPS):
-            if s + 2 < N_GROUPS:
-                transposes(s + 2)
+            ahead = s + 2 < N_GROUPS
+            o_sb = res.tile([P, PASSES * K], F32, tag="o_sb")
             if s + 1 < N_GROUPS:
                 quantise(s + 1)
-            if s + 2 < N_GROUPS:
-                copies(s + 2, (0, 1), False)
-            o_sb = res.tile([P, PASSES * K], F32, tag="o_sb")
-            one_pass(s, 0, o_sb, nc.scalar.copy)
-            one_pass(s, 1, o_sb, nc.vector.tensor_copy)
-            if s + 2 < N_GROUPS:
-                copies(s + 2, (2, 3), False)
-            base = s * PASSES * K
-            half = PASSES * K // 2
-            for m in range(2, PASSES):
+            for m in range(0, 4):
                 one_pass(s, m, o_sb, nc.scalar.copy)
-                if s >= N_GROUPS - 2 and m == PASSES // 2 - 1:
-                    nc.sync.dma_start(out=out_view[:, base : base + half], in_=o_sb[:, 0:half])
+            if ahead:
+                transposes(s + 2, (0, 1))
+                copies(s + 2, (0, 1), False)
+            half = PASSES * K // 2
             if s >= N_GROUPS - 2:
-                nc.sync.dma_start(out=out_view[:, base + half : base + 2 * half], in_=o_sb[:, half : 2 * half])
+                nc.sync.dma_start(out=out_view[s, :, 0:half], in_=o_sb[:, 0:half])
+            for m in range(4, PASSES):
+                one_pass(s, m, o_sb, nc.vector.tensor_copy if m == VECTOR_PASS else nc.scalar.copy)
+            if ahead:
+                transposes(s + 2, (2, 3))
+                copies(s + 2, (2, 3), False)
+            if s >= N_GROUPS - 2:
+                nc.sync.dma_start(out=out_view[s, :, half : 2 * half], in_=o_sb[:, half : 2 * half])
             else:
-                nc.sync.dma_start(out=out_view[:, base : base + 2 * half], in_=o_sb[:])
+                nc.sync.dma_start(out=out_view[s], in_=o_sb[:])

@@ -40,7 +40,7 @@ def tile_patch_expanding_t_kernel(tc, x, w, grad_out, out):
         ctx.enter_context(tc.manual_schedule())
 
         w_sb = keep.tile([P, 4 * K], BF16, name="w_sb")
-        nc.sync.dma_start(out=w_sb[:], in_=w_view)
+        nc.scalar.dma_start(out=w_sb[:], in_=w_view)
         g_tiles = {}
         for g_first, g_end in LOAD_CUTS:
             g_sb = keep.tile([P, g_end - g_first, RUN * K], BF16, name="g_sb_%d" % g_first)

from contextlib import ExitStack

import concourse.mybir as mybir
from concourse.masks import make_identity

F32 = mybir.dt.float32
BF16 = mybir.dt.bfloat16
U32 = mybir.dt.uint32
U8 = mybir.dt.uint8
E4M3X4 = mybir.dt.float8_e4m3fn_x4
E5M2X4 = mybir.dt.float8_e5m2_x4

P = 128
K = 512
TOKENS = 8192
T_PER_P = 32
GROUP_T = 4
N_GROUPS = T_PER_P // GROUP_T
VECTOR_PASS = 5
PASSES = 2 * GROUP_T
RUN = 2 * GROUP_T
LOAD_CUTS = ((0, 1), (1, 2), (2, 3), (3, 5), (5, 8))

FLOPS = 2 * TOKENS * K * K
BYTES = TOKENS * K * 2 + K * K * 2 + TOKENS * K * 4


def tile_patch_expanding_t_kernel(tc, x, w, grad_out, out):
    nc = tc.nc
    g_view = grad_out.rearrange("b (g p t) k -> (b p) g (t k)", p=P, t=RUN)
    out_view = out.rearrange("b (g p t) c -> g (b p) (t c)", p=P, t=GROUP_T)
    w_view = w.rearrange("(p a) k -> p (a k)", a=4)

    with ExitStack() as ctx:
        keep = ctx.enter_context(tc.tile_pool(name="keep", bufs=1))
        stage = ctx.enter_context(tc.tile_pool(name="stage", bufs=3))
        res = ctx.enter_context(tc.tile_pool(name="res", bufs=6))
        tp_pool = ctx.enter_context(tc.psum_pool(name="tp", bufs=4))
        acc_pool = ctx.enter_context(tc.psum_pool(name="acc", bufs=4))
        ctx.enter_context(tc.manual_schedule())

        w_sb = keep.tile([P, 4 * K], BF16, name="w_sb")
        nc.scalar.dma_start(out=w_sb[:], in_=w_view)
        g_tiles = {}
        for g_first, g_end in LOAD_CUTS:
            g_sb = keep.tile([P, g_end - g_first, RUN * K], BF16, name="g_sb_%d" % g_first)
            nc.sync.dma_start(out=g_sb[:], in_=g_view[:, g_first:g_end, :])
            for g in range(g_first, g_end):
                g_tiles[g] = g_sb[:, g - g_first, :].bitcast(F32)

        ident = keep.tile([P, P], F32, name="ident")
        make_identity(nc, ident[:])

        perm = keep.tile([P, P], F32, name="perm")
        nc.vector.tensor_copy(
            out=perm[:].rearrange("p (r i j) -> p r i j", r=2, i=8),
            in_=ident[:].rearrange("p (i r j) -> p r i j", i=8, r=2),
        )

        def regroup(copy, bank, grouped, b, m):
            dst = grouped[:].bitcast(F32).rearrange("p (m n v) -> p m n v", m=m, v=4)
            src = bank[:].rearrange("p v (r n) -> p r n v", r=2)
            copy(out=dst[:, 2 * b : 2 * b + 2, :, :], in_=src)

        w_words = w_sb[:].bitcast(F32)
        w_grouped = keep.tile([P, 4 * K], BF16, name="w_grouped", align_bytes=64)
        w_codes = keep.tile([P, K], U32, name="w_codes", align_bytes=64)
        w_scales = keep.tile([P, K], U8, name="w_scales", align_bytes=64)
        for b in range(2):
            bank = tp_pool.tile([P, 4, P], F32, tag="tp")
            for j in range(4):
                col = (4 * b + j) * P
                nc.tensor.transpose(bank[:, j, :], w_words[:, col : col + P], ident[:])
            nc.vector.tensor_copy(
                out=w_grouped[:].bitcast(F32).rearrange("p (n a u) -> p n a u", a=4, u=2)[:, :, 2 * b : 2 * b + 2, :],
                in_=bank[:].rearrange("p (m u) n -> p n m u", u=2),
            )
        nc.vector.quantize_mx(out=w_codes[:].bitcast(E4M3X4), scales=w_scales[:], in_=w_grouped[:])

        banks = {}
        grouped = {}
        codes = {}
        scales = {}

        def transposes(g, bs):
            for b in bs:
                bank = tp_pool.tile([P, 4, P], F32, tag="tp")
                for h in range(2):
                    for u in range(2):
                        col = (GROUP_T * h + b) * (K // 2) + P * u
                        nc.tensor.transpose(bank[:, 2 * h + u, :], g_tiles[g][:, col : col + P], perm[:])
                banks[(g, b)] = bank

        def copies(g, bs, both):
            if g not in grouped:
                grouped_t = stage.tile([P, PASSES * K], BF16, tag="grouped", align_bytes=64)
                grouped[g] = grouped_t
            for b in bs:
                copy = nc.scalar.copy if (both and b % 2 == 1) else nc.vector.tensor_copy
                regroup(copy, banks[(g, b)], grouped[g], b, PASSES)

        def quantise(g):
            codes_t = stage.tile([P, PASSES * P], U32, tag="codes", align_bytes=64)
            scales_t = stage.tile([P, PASSES * P], U8, tag="scales", align_bytes=64)
            nc.vector.quantize_mx(out=codes_t[:].bitcast(E5M2X4), scales=scales_t[:], in_=grouped[g][:])
            codes[g] = codes_t
            scales[g] = scales_t

        def one_pass(g, m, o_sb, copy):
            acc = acc_pool.tile([P, K], F32, tag="acc")
            cols = slice(m * P, (m + 1) * P)
            nc.tensor.matmul_mx(
                out=acc[:],
                lhsT=codes[g][:, cols].bitcast(E5M2X4),
                lhsT_scale=scales[g][:, cols],
                rhs=w_codes[:].bitcast(E4M3X4),
                rhs_scale=w_scales[:],
                start=True,
                stop=True,
            )
            copy(out=o_sb[:, m * K : (m + 1) * K], in_=acc[:])

        transposes(0, range(4))
        copies(0, range(4), True)
        transposes(1, range(4))
        quantise(0)
        copies(1, range(4), True)

        for s in range(N_GROUPS):
            ahead = s + 2 < N_GROUPS
            o_sb = res.tile([P, PASSES * K], F32, tag="o_sb")
            if s + 1 < N_GROUPS:
                quantise(s + 1)
            for m in range(0, 4):
                one_pass(s, m, o_sb, nc.scalar.copy)
            if ahead:
                transposes(s + 2, (0, 1))
                copies(s + 2, (0, 1), False)
            half = PASSES * K // 2
            if s >= N_GROUPS - 2:
                nc.sync.dma_start(out=out_view[s, :, 0:half], in_=o_sb[:, 0:half])
            for m in range(4, PASSES):
                one_pass(s, m, o_sb, nc.vector.tensor_copy if m == VECTOR_PASS else nc.scalar.copy)
            if ahead:
                transposes(s + 2, (2, 3))
                copies(s + 2, (2, 3), False)
            if s >= N_GROUPS - 2:
                nc.sync.dma_start(out=out_view[s, :, half : 2 * half], in_=o_sb[:, half : 2 * half])
            else:
                nc.sync.dma_start(out=out_view[s], in_=o_sb[:])
